import numpy as np
import ml_dtypes


def mxq(x, axis, fmt="e4m3"):
    dtype, down = {"e4m3": (ml_dtypes.float8_e4m3fn, 7), "e5m2": (ml_dtypes.float8_e5m2, 14)}[fmt]
    v = np.moveaxis(np.asarray(x, np.float32).astype(ml_dtypes.bfloat16).astype(np.float64), axis, -1)
    blocks = v.reshape(v.shape[:-1] + (-1, 32))
    amax = np.abs(blocks).max(-1, keepdims=True)
    byte = np.maximum(np.where(amax > 0, np.frexp(amax)[1] - 1 + 127, 0) - down, 1)
    scale = np.exp2(byte - 127.0)
    codes = (blocks / scale).astype(np.float32).astype(dtype).astype(np.float64)
    return np.moveaxis((codes * scale).reshape(v.shape), -1, axis)


WIDE = False


def mx_kscale(k):
    if not WIDE:
        return np.ones(k)
    levels = np.array([10, -10, 5, -5, 0])
    if k % 512:
        return np.exp2(np.random.permutation(np.resize(levels, k // 32))).repeat(32)
    a = np.empty((k // 512, 16))
    for p in range(k // 512):
        a[p, :8] = np.random.permutation(np.resize(levels, 8))
        for g in range(8):
            far = levels[np.abs(levels - a[p, g]) >= 10]
            a[p, g + 8] = far[np.random.randint(len(far))]
    return np.exp2(a.ravel()).repeat(32)


BF16 = ml_dtypes.bfloat16


def bf(x):
    return np.asarray(x, np.float32).astype(BF16)


def f64(x):
    return np.asarray(x).astype(np.float64)


WAY, SHOT, QUERY_SHOT, D, M = 8, 8, 8, 256, 512
G, Q = 4, 5
NS, NQ = WAY * SHOT, WAY * QUERY_SHOT


def log_softmax(v, axis):
    z = v - v.max(axis, keepdims=True)
    return z - np.log(np.exp(z).sum(axis, keepdims=True))


def setup_inputs():
    s = mx_kscale(M)
    return {"feature_map": bf(np.random.standard_normal((NS + NQ, D, M)) * np.sqrt(M) * s),
            "weight2": bf(np.random.uniform(0.0, 1.0, (NS, NQ, M)) / s),
            "scale": bf(G * Q * Q * SHOT / np.sqrt(D) * (1.0 + 0.1 * np.random.standard_normal(1)))}


def reference(feature_map, weight2, scale):
    fq = mxq(f64(feature_map), 2, "e4m3")
    wq = mxq(f64(weight2), 2, "e4m3")
    support = fq[:NS]
    query = fq[NS:]
    centroid = (wq @ support.transpose(0, 2, 1)) / M
    query_r = (wq.transpose(1, 0, 2) @ query.transpose(0, 2, 1)).transpose(1, 0, 2) / M
    l2 = ((centroid - query_r) ** 2).sum(-1)
    neg_l2 = -l2.T
    logits = neg_l2 / (G * Q * Q * SHOT) * f64(scale)
    return log_softmax(logits, 1)

@@ -1,0 +1,298 @@
+from contextlib import ExitStack
+
+import concourse.mybir as mybir
+from concourse.masks import make_identity
+
+F32 = mybir.dt.float32
+BF16 = mybir.dt.bfloat16
+U32 = mybir.dt.uint32
+U8 = mybir.dt.uint8
+I32 = mybir.dt.int32
+FP8X4 = mybir.dt.float8_e4m3fn_x4
+ACT = mybir.ActivationFunctionType
+ALU = mybir.AluOpType
+AX = mybir.AxisListType
+
+P = 128
+NS = 64
+NQ = 64
+D = 256
+M = 512
+FLOPS = 2 * 2 * NS * NQ * D * M
+
+IMG = 4
+NSTEP = (NS + NQ) // IMG
+HALF = NS // IMG
+LOOKAHEAD = 5
+PIN = True
+WIDTHS = (128, 128, 128, 128, 128, 128, 128, 64)
+
+
+def tile_proto_t_kernel(tc, feature_map, weight2, scale, out):
+    nc = tc.nc
+    with ExitStack() as ctx:
+        const = ctx.enter_context(tc.tile_pool(name="const", bufs=1))
+        xpool = ctx.enter_context(tc.tile_pool(name="xpool", bufs=LOOKAHEAD + 1))
+        wpool = ctx.enter_context(tc.tile_pool(name="wpool", bufs=LOOKAHEAD + 1))
+        work = ctx.enter_context(tc.tile_pool(name="work", bufs=3))
+        psum = ctx.enter_context(tc.psum_pool(name="psum", bufs=2))
+
+        ident = const.tile([P, P], F32)
+        make_identity(nc, ident[:])
+        sc_bf = const.tile([P, 1], BF16)
+        nc.scalar.dma_start(out=sc_bf[:], in_=scale.partition_broadcast(P))
+        a_sb = const.tile([P, 1], F32)
+        nc.vector.tensor_scalar_mul(a_sb[:], sc_bf[:], -1.0 / (800.0 * M * M))
+        l2col = const.tile([P, P], F32)
+        nc.vector.memset(l2col[:], 0.0)
+        warm = const.tile([P, 1], F32)
+        nc.scalar.activation(out=warm[:], in_=l2col[:, 0:1], func=ACT.Exp)
+
+        csb = const.tile([P, 2 * NQ * NS], F32)
+        csb4 = csb[:].rearrange("p (j q s) -> p j q s", j=2, q=NQ, s=NS)
+        gb = const.tile([P, NQ * NS * 4], BF16, align_bytes=64)
+        gb5 = gb[:].bitcast(F32).rearrange("p (b r s u) -> p b r s u", b=NQ // 2, r=2, s=NS, u=2)
+        wbc = const.tile([P, NQ * NS + 64], U32, align_bytes=64)
+        wbs = const.tile([P, NQ * NS + 64], U8, align_bytes=64)
+        wac = const.tile([P, NQ * NS + 64], U32, align_bytes=64)
+        was = const.tile([P, NQ * NS + 64], U8, align_bytes=64)
+        for pad in (wbc, wbs, wac, was):
+            nc.vector.memset(pad[:, NQ * NS : NQ * NS + 64].bitcast(I32), 0)
+
+
+        xs = {}
+        ws = {}
+        xt = {}
+        wt = {}
+        gx = {}
+        ga = {}
+        xc = {}
+        xsc = {}
+        mm = {}
+        diff = {}
+        dt = {}
+
+        def load(g):
+            if g >= NSTEP:
+                return
+            xs[g] = xpool.tile([P, IMG * 1024], BF16, name="xs", tag="xs")
+            dst = xs[g][:].rearrange("p (b f) -> p b f", b=IMG)
+            src = (
+                feature_map[IMG * g : IMG * (g + 1)]
+                .rearrange("i d m -> (i d) m")
+                .rearrange("(p b r) m -> p b (r m)", b=IMG, r=2)
+            )
+            if g == 0:
+                nc.sync.dma_start(out=dst[:, 0, :], in_=src[:, 0, :])
+            if g < HALF:
+                ws[g] = wpool.tile([P, 2 * M], BF16, name="ws", tag="ws")
+                nc.sync.dma_start(
+                    out=ws[g][:],
+                    in_=weight2[IMG * g : IMG * (g + 1)].rearrange("s q m -> (s q) m").rearrange("(p r) m -> p (r m)", r=2),
+                )
+            if g == 0:
+                for i in range(1, IMG):
+                    nc.sync.dma_start(out=dst[:, i, :], in_=src[:, i, :])
+            else:
+                nc.sync.dma_start(
+                    out=xs[g][:],
+                    in_=feature_map[IMG * g : IMG * (g + 1)]
+                    .rearrange("i d m -> (i d) m")
+                    .rearrange("(p r) m -> p (r m)", r=2 * IMG),
+                )
+
+        def transp_w(g):
+            if g >= HALF:
+                return
+            wt[g] = psum.tile([P, 2, 256], F32, name="wt", tag="aux", bufs=2)
+            ww = ws[g][:].bitcast(F32)
+            for t in range(2):
+                for u in range(2):
+                    nc.tensor.transpose(
+                        wt[g][:, u, t * P : (t + 1) * P], ww[:, t * 256 + u : (t + 1) * 256 : 2], ident[:]
+                    )
+
+        def transp_x(g, i):
+            if g >= NSTEP:
+                return
+            xw = xs[g][:].bitcast(F32)
+            xt[g, i] = psum.tile([P, 2, IMG, 2, 32], F32, name="xt", tag="xt", bufs=4)
+            for j in range(2):
+                for u in range(2):
+                    c0 = i * 512 + j * 256
+                    nc.tensor.transpose(
+                        xt[g, i][:, u, :, j, :], xw[:, c0 + u : c0 + 256 : 2], ident[:].rearrange("p (i c) -> p i c", i=IMG)
+                    )
+
+        def copy_x(g, i, on_vector):
+            dst = gx[g][:].bitcast(F32).rearrange("p (i b c u) -> p i b c u", i=IMG, b=IMG, c=64, u=2)[:, :, i, :, :]
+            src = xt[g, i][:].rearrange("p u i r c -> p i (r c) u")
+            if on_vector:
+                nc.vector.tensor_copy(out=dst, in_=src)
+            else:
+                nc.scalar.copy(out=dst, in_=src)
+
+        def copies_w(g):
+            if g < 0 or g >= HALF:
+                return
+            ga[g] = work.tile([P, 1024], BF16, name="ga", tag="ga", align_bytes=64)
+            nc.vector.tensor_copy(
+                out=ga[g][:].bitcast(F32).rearrange("p (c r u) -> p c r u", r=2, u=2),
+                in_=wt[g][:].rearrange("p u (r c) -> p c r u", r=2),
+            )
+            nc.vector.tensor_copy(
+                out=gb5[:, :, :, IMG * g : IMG * (g + 1), :],
+                in_=wt[g][:].rearrange("p u (r s b) -> p b r s u", r=2, s=IMG),
+            )
+
+        def copies_x(g):
+            if g >= NSTEP:
+                return
+            gx[g] = work.tile([P, IMG * 1024], BF16, name="gx", tag="gx", align_bytes=64)
+            for i in range(IMG):
+                if g == NSTEP - 1:
+                    copy_x(g, i, i % 2 == 1)
+                else:
+                    copy_x(g, i, g >= HALF and i == IMG - 1)
+
+        def quant_wa(g):
+            if g < 0 or g >= HALF:
+                return
+            nc.vector.quantize_mx(
+                out=wac[:, 256 * g : 256 * (g + 1)].bitcast(FP8X4), scales=was[:, 256 * g : 256 * (g + 1)], in_=ga[g][:]
+            )
+
+        def quant_wb(k):
+            nc.vector.quantize_mx(
+                out=wbc[:, k * 1024 : (k + 1) * 1024].bitcast(FP8X4),
+                scales=wbs[:, k * 1024 : (k + 1) * 1024],
+                in_=gb[:, k * 4096 : (k + 1) * 4096],
+            )
+
+        def quant_x(g):
+            if g < 0 or g >= NSTEP:
+                return
+            xc[g] = work.tile([P, IMG * 256], U32, name="xc", tag="xc", align_bytes=64)
+            xsc[g] = work.tile([P, IMG * 256], U8, name="xsc", tag="xsc", align_bytes=64)
+            pieces = 1
+            wid = IMG * 256 // pieces
+            for h in range(pieces):
+                nc.vector.quantize_mx(
+                    out=xc[g][:, h * wid : (h + 1) * wid].bitcast(FP8X4),
+                    scales=xsc[g][:, h * wid : (h + 1) * wid],
+                    in_=gx[g][:, 4 * h * wid : 4 * (h + 1) * wid],
+                )
+
+        def mx(g):
+            if g < 0 or g >= NSTEP:
+                return
+            mm[g] = psum.tile([P, 512], F32, name="mm", tag="mm", bufs=2)
+            for slot in range(8):
+                if g < HALF:
+                    j, i = slot // IMG, slot % IMG
+                    codes, planes = wac, was
+                else:
+                    i, j = (slot // 4) * 2 + slot % 2, (slot // 2) % 2
+                    codes, planes = wbc, wbs
+                c0 = i * 256 + j * P
+                w0 = (IMG * (g % HALF) + i) * 64
+                n = WIDTHS[slot]
+                nc.tensor.matmul_mx(
+                    out=mm[g][:, slot * 64 : slot * 64 + n],
+                    lhsT=xc[g][:, c0 : c0 + P].bitcast(FP8X4),
+                    lhsT_scale=xsc[g][:, c0 : c0 + P],
+                    rhs=codes[:, w0 : w0 + n].bitcast(FP8X4),
+                    rhs_scale=planes[:, w0 : w0 + n],
+                    start=True,
+                    stop=True,
+                )
+
+        def ccopy(g):
+            if g < 0 or g >= HALF:
+                return
+            nc.scalar.copy(
+                out=csb4[:, :, :, IMG * g : IMG * (g + 1)],
+                in_=mm[g][:].rearrange("p (j i q) -> p j q i", j=2, i=IMG, q=NQ),
+            )
+
+        def sub(g):
+            if g < HALF or g >= NSTEP:
+                return
+            h = g - HALF
+            diff[g] = work.tile([P, 512], F32, name="diff", tag="diff")
+            nc.vector.tensor_tensor(
+                out=diff[g][:].rearrange("p (a j f) -> p a j f", a=2, j=2),
+                in0=mm[g][:].rearrange("p (a j f) -> p a j f", a=2, j=2),
+                in1=csb4[:, :, IMG * h : IMG * (h + 1), :].rearrange("p j (a b) s -> p a j (b s)", a=2, b=2),
+                op=ALU.subtract,
+            )
+
+        def dtr(g):
+            if g < HALF or g >= NSTEP:
+                return
+            dt[g] = psum.tile([P, 512], F32, name="dt", tag="aux", bufs=2)
+            for b in range(4):
+                nc.tensor.transpose(dt[g][:, b * P : (b + 1) * P], diff[g][:, b * P : (b + 1) * P], ident[:])
+
+        def sq(g):
+            if g < HALF or g >= NSTEP:
+                return
+            h = g - HALF
+            for a in range(2):
+                junk = work.tile([P, 256], F32, name="junk", tag="junk")
+                nc.scalar.activation(
+                    out=junk[:],
+                    in_=dt[g][:, a * 256 : (a + 1) * 256],
+                    func=ACT.Square,
+                    accum_out=l2col[:, 2 * h + a : 2 * h + a + 1],
+                )
+
+        if PIN:
+            ctx.enter_context(tc.manual_schedule())
+
+        for g in range(LOOKAHEAD):
+            load(g)
+        for k in range(NSTEP + 6):
+            load(k + LOOKAHEAD)
+            copies_w(k - 1)
+            sub(k - 3)
+            quant_x(k - 1)
+            quant_wa(k - 1)
+            if k == HALF + 1:
+                quant_wb(0)
+            if k in (HALF + 4, HALF + 8, HALF + 12):
+                quant_wb((k - HALF) // 4)
+            sq(k - 5)
+            ccopy(k - 3)
+            dtr(k - 4)
+            if k == 0:
+                transp_x(0, 0)
+            transp_w(k)
+            for i in range(1 if k == 0 else 0, IMG):
+                transp_x(k, i)
+            mx(k - 2)
+            copies_x(k)
+
+        l2t = psum.tile([P, P], F32, name="l2t", tag="aux", bufs=2)
+        nc.tensor.transpose(l2t[:], l2col[:], ident[:])
+        lg = const.tile([P, 2, NS], F32)
+        nc.vector.tensor_scalar_mul(lg[:].rearrange("p a s -> p (a s)"), l2t[:], a_sb[:, 0:1])
+        top = const.tile([P, 2], F32)
+        nc.vector.tensor_reduce(out=top[:], in_=lg[:], axis=AX.X, op=ALU.max)
+        z = const.tile([P, 2, NS], F32)
+        nc.vector.tensor_tensor(
+            out=z[:], in0=lg[:], in1=top[:].unsqueeze(2).to_broadcast([P, 2, NS]), op=ALU.subtract
+        )
+        ez = const.tile([P, 2, NS], F32)
+        tot = const.tile([P, 2], F32)
+        for a in range(2):
+            nc.scalar.activation(out=ez[:, a, :], in_=z[:, a, :], func=ACT.Exp, accum_out=tot[:, a : a + 1])
+        ltot = const.tile([P, 2], F32)
+        nc.scalar.activation(out=ltot[:], in_=tot[:], func=ACT.Ln)
+        res = const.tile([P, 2, NS], F32)
+        nc.vector.tensor_tensor(
+            out=res[:], in0=z[:], in1=ltot[:].unsqueeze(2).to_broadcast([P, 2, NS]), op=ALU.subtract
+        )
+        nc.sync.dma_start(
+            out=out.rearrange("(u a) s -> u (a s)", a=2), in_=res[0:32].rearrange("p a s -> p (a s)")
+        )

@@ -24,6 +24,7 @@ IMG = 4
 NSTEP = (NS + NQ) // IMG
 HALF = NS // IMG
 LOOKAHEAD = 5
+SPLIT = (1, 3)
 PIN = True
 WIDTHS = (128, 128, 128, 128, 128, 128, 128, 64)
 
@@ -33,6 +34,7 @@ def tile_proto_t_kernel(tc, feature_map, weight2, scale, out):
     with ExitStack() as ctx:
         const = ctx.enter_context(tc.tile_pool(name="const", bufs=1))
         xpool = ctx.enter_context(tc.tile_pool(name="xpool", bufs=LOOKAHEAD + 1))
+        dpool = ctx.enter_context(tc.tile_pool(name="dpool", bufs=3))
         wpool = ctx.enter_context(tc.tile_pool(name="wpool", bufs=LOOKAHEAD + 1))
         work = ctx.enter_context(tc.tile_pool(name="work", bufs=3))
         psum = ctx.enter_context(tc.psum_pool(name="psum", bufs=2))
@@ -50,17 +52,18 @@ def tile_proto_t_kernel(tc, feature_map, weight2, scale, out):
 
         csb = const.tile([P, 2 * NQ * NS], F32)
         csb4 = csb[:].rearrange("p (j q s) -> p j q s", j=2, q=NQ, s=NS)
-        gb = const.tile([P, NQ * NS * 4], BF16, align_bytes=64)
-        gb5 = gb[:].bitcast(F32).rearrange("p (b r s u) -> p b r s u", b=NQ // 2, r=2, s=NS, u=2)
-        wbc = const.tile([P, NQ * NS + 64], U32, align_bytes=64)
-        wbs = const.tile([P, NQ * NS + 64], U8, align_bytes=64)
+        wqc = [const.tile([P, IMG * NS + 64], U32, name=f"wqc{b}", align_bytes=64) for b in range(2)]
+        wqs = [const.tile([P, IMG * NS + 64], U8, name=f"wqs{b}", align_bytes=64) for b in range(2)]
         wac = const.tile([P, NQ * NS + 64], U32, align_bytes=64)
         was = const.tile([P, NQ * NS + 64], U8, align_bytes=64)
-        for pad in (wbc, wbs, wac, was):
+        for pad in (wac, was):
             nc.vector.memset(pad[:, NQ * NS : NQ * NS + 64].bitcast(I32), 0)
+        for pad in wqc + wqs:
+            nc.vector.memset(pad[:, IMG * NS : IMG * NS + 64].bitcast(I32), 0)
 
 
         xs = {}
+        xd = {}
         ws = {}
         xt = {}
         wt = {}
@@ -120,9 +123,23 @@ def tile_proto_t_kernel(tc, feature_map, weight2, scale, out):
             for j in range(2):
                 for u in range(2):
                     c0 = i * 512 + j * 256
+                    if (g, i) in xd:
+                        words = xd[g, i][:, (2 * j + u) * P : (2 * j + u + 1) * P]
+                    else:
+                        words = xw[:, c0 + u : c0 + 256 : 2]
                     nc.tensor.transpose(
-                        xt[g, i][:, u, :, j, :], xw[:, c0 + u : c0 + 256 : 2], ident[:].rearrange("p (i c) -> p i c", i=IMG)
+                        xt[g, i][:, u, :, j, :], words, ident[:].rearrange("p (i c) -> p i c", i=IMG)
                     )
+
+        def split_x(g):
+            if g < 1 or g >= NSTEP:
+                return
+            for i in SPLIT:
+                xd[g, i] = dpool.tile([P, 512], F32, name="xd", tag=f"xd{i}")
+                nc.vector.tensor_copy(
+                    out=xd[g, i][:].rearrange("p (j u w) -> p j u w", j=2, u=2),
+                    in_=xs[g][:, i * 1024 : (i + 1) * 1024].bitcast(F32).rearrange("p (j w u) -> p j u w", j=2, u=2),
+                )
 
         def copy_x(g, i, on_vector):
             dst = gx[g][:].bitcast(F32).rearrange("p (i b c u) -> p i b c u", i=IMG, b=IMG, c=64, u=2)[:, :, i, :, :]
@@ -140,10 +157,6 @@ def tile_proto_t_kernel(tc, feature_map, weight2, scale, out):
                 out=ga[g][:].bitcast(F32).rearrange("p (c r u) -> p c r u", r=2, u=2),
                 in_=wt[g][:].rearrange("p u (r c) -> p c r u", r=2),
             )
-            nc.vector.tensor_copy(
-                out=gb5[:, :, :, IMG * g : IMG * (g + 1), :],
-                in_=wt[g][:].rearrange("p u (r s b) -> p b r s u", r=2, s=IMG),
-            )
 
         def copies_x(g):
             if g >= NSTEP:
@@ -153,7 +166,7 @@ def tile_proto_t_kernel(tc, feature_map, weight2, scale, out):
                 if g == NSTEP - 1:
                     copy_x(g, i, i % 2 == 1)
                 else:
-                    copy_x(g, i, g >= HALF and i == IMG - 1)
+                    copy_x(g, i, False)
 
         def quant_wa(g):
             if g < 0 or g >= HALF:
@@ -162,11 +175,17 @@ def tile_proto_t_kernel(tc, feature_map, weight2, scale, out):
                 out=wac[:, 256 * g : 256 * (g + 1)].bitcast(FP8X4), scales=was[:, 256 * g : 256 * (g + 1)], in_=ga[g][:]
             )
 
-        def quant_wb(k):
-            nc.vector.quantize_mx(
-                out=wbc[:, k * 1024 : (k + 1) * 1024].bitcast(FP8X4),
-                scales=wbs[:, k * 1024 : (k + 1) * 1024],
-                in_=gb[:, k * 4096 : (k + 1) * 4096],
+        def move_w(g):
+            if g < HALF or g >= NSTEP:
+                return
+            h = g - HALF
+            nc.vector.tensor_copy(
+                out=wqc[h % 2][:, 0 : IMG * NS].bitcast(I32).rearrange("p (q s) -> p q s", q=IMG),
+                in_=wac[:, 0 : NS * NQ].bitcast(I32).rearrange("p (s q) -> p q s", s=NS)[:, IMG * h : IMG * (h + 1), :],
+            )
+            nc.vector.tensor_copy(
+                out=wqs[h % 2][:, 0 : IMG * NS].rearrange("p (q s) -> p q s", q=IMG),
+                in_=was[:, 0 : NS * NQ].rearrange("p (s q) -> p q s", s=NS)[:, IMG * h : IMG * (h + 1), :],
             )
 
         def quant_x(g):
@@ -191,11 +210,12 @@ def tile_proto_t_kernel(tc, feature_map, weight2, scale, out):
                 if g < HALF:
                     j, i = slot // IMG, slot % IMG
                     codes, planes = wac, was
+                    w0 = (IMG * g + i) * 64
                 else:
                     i, j = (slot // 4) * 2 + slot % 2, (slot // 2) % 2
-                    codes, planes = wbc, wbs
+                    codes, planes = wqc[g % 2], wqs[g % 2]
+                    w0 = i * 64
                 c0 = i * 256 + j * P
-                w0 = (IMG * (g % HALF) + i) * 64
                 n = WIDTHS[slot]
                 nc.tensor.matmul_mx(
                     out=mm[g][:, slot * 64 : slot * 64 + n],
@@ -255,13 +275,11 @@ def tile_proto_t_kernel(tc, feature_map, weight2, scale, out):
         for k in range(NSTEP + 6):
             load(k + LOOKAHEAD)
             copies_w(k - 1)
+            split_x(k + 1)
             sub(k - 3)
             quant_x(k - 1)
             quant_wa(k - 1)
-            if k == HALF + 1:
-                quant_wb(0)
-            if k in (HALF + 4, HALF + 8, HALF + 12):
-                quant_wb((k - HALF) // 4)
+            move_w(k - 1)
             sq(k - 5)
             ccopy(k - 3)
             dtr(k - 4)

@@ -24,18 +24,15 @@ IMG = 4
 NSTEP = (NS + NQ) // IMG
 HALF = NS // IMG
 LOOKAHEAD = 5
-SPLIT = (1, 3)
-PIN = True
-WIDTHS = (128, 128, 128, 128, 128, 128, 128, 64)
 
 
 def tile_proto_t_kernel(tc, feature_map, weight2, scale, out):
     nc = tc.nc
     with ExitStack() as ctx:
         const = ctx.enter_context(tc.tile_pool(name="const", bufs=1))
-        xpool = ctx.enter_context(tc.tile_pool(name="xpool", bufs=LOOKAHEAD + 1))
+        xpool = ctx.enter_context(tc.tile_pool(name="xpool", bufs=LOOKAHEAD + 2))
         dpool = ctx.enter_context(tc.tile_pool(name="dpool", bufs=3))
-        wpool = ctx.enter_context(tc.tile_pool(name="wpool", bufs=LOOKAHEAD + 1))
+        wpool = ctx.enter_context(tc.tile_pool(name="wpool", bufs=LOOKAHEAD + 2))
         work = ctx.enter_context(tc.tile_pool(name="work", bufs=3))
         psum = ctx.enter_context(tc.psum_pool(name="psum", bufs=2))
 
@@ -43,8 +40,6 @@ def tile_proto_t_kernel(tc, feature_map, weight2, scale, out):
         make_identity(nc, ident[:])
         sc_bf = const.tile([P, 1], BF16)
         nc.scalar.dma_start(out=sc_bf[:], in_=scale.partition_broadcast(P))
-        a_sb = const.tile([P, 1], F32)
-        nc.vector.tensor_scalar_mul(a_sb[:], sc_bf[:], -1.0 / (800.0 * M * M))
         l2col = const.tile([P, P], F32)
         nc.vector.memset(l2col[:], 0.0)
         warm = const.tile([P, 1], F32)
@@ -52,15 +47,14 @@ def tile_proto_t_kernel(tc, feature_map, weight2, scale, out):
 
         csb = const.tile([P, 2 * NQ * NS], F32)
         csb4 = csb[:].rearrange("p (j q s) -> p j q s", j=2, q=NQ, s=NS)
-        wqc = [const.tile([P, IMG * NS + 64], U32, name=f"wqc{b}", align_bytes=64) for b in range(2)]
-        wqs = [const.tile([P, IMG * NS + 64], U8, name=f"wqs{b}", align_bytes=64) for b in range(2)]
-        wac = const.tile([P, NQ * NS + 64], U32, align_bytes=64)
-        was = const.tile([P, NQ * NS + 64], U8, align_bytes=64)
-        for pad in (wac, was):
-            nc.vector.memset(pad[:, NQ * NS : NQ * NS + 64].bitcast(I32), 0)
-        for pad in wqc + wqs:
-            nc.vector.memset(pad[:, IMG * NS : IMG * NS + 64].bitcast(I32), 0)
-
+        wac = const.tile([P, NQ * NS], U32, align_bytes=64)
+        was = const.tile([P, NQ * NS], U8, align_bytes=64)
+        wqc0 = const.tile([P, 2 * IMG * NS], U32, align_bytes=64)
+        wqs0 = const.tile([P, 2 * IMG * NS], U8, align_bytes=64)
+        wqc1 = const.tile([P, 2 * IMG * NS], U32, align_bytes=64)
+        wqs1 = const.tile([P, 2 * IMG * NS], U8, align_bytes=64)
+        wqc = (wqc0, wqc1)
+        wqs = (wqs0, wqs1)
 
         xs = {}
         xd = {}
@@ -80,11 +74,8 @@ def tile_proto_t_kernel(tc, feature_map, weight2, scale, out):
                 return
             xs[g] = xpool.tile([P, IMG * 1024], BF16, name="xs", tag="xs")
             dst = xs[g][:].rearrange("p (b f) -> p b f", b=IMG)
-            src = (
-                feature_map[IMG * g : IMG * (g + 1)]
-                .rearrange("i d m -> (i d) m")
-                .rearrange("(p b r) m -> p b (r m)", b=IMG, r=2)
-            )
+            rows = feature_map[IMG * g : IMG * (g + 1)].rearrange("i d m -> (i d) m")
+            src = rows.rearrange("(p b r) m -> p b (r m)", b=IMG, r=2)
             if g == 0:
                 nc.sync.dma_start(out=dst[:, 0, :], in_=src[:, 0, :])
             if g < HALF:
@@ -97,15 +88,10 @@ def tile_proto_t_kernel(tc, feature_map, weight2, scale, out):
                 for i in range(1, IMG):
                     nc.sync.dma_start(out=dst[:, i, :], in_=src[:, i, :])
             else:
-                nc.sync.dma_start(
-                    out=xs[g][:],
-                    in_=feature_map[IMG * g : IMG * (g + 1)]
-                    .rearrange("i d m -> (i d) m")
-                    .rearrange("(p r) m -> p (r m)", r=2 * IMG),
-                )
+                nc.sync.dma_start(out=xs[g][:], in_=rows.rearrange("(p r) m -> p (r m)", r=2 * IMG))
 
         def transp_w(g):
-            if g >= HALF:
+            if g < 0 or g >= HALF:
                 return
             wt[g] = psum.tile([P, 2, 256], F32, name="wt", tag="aux", bufs=2)
             ww = ws[g][:].bitcast(F32)
@@ -115,33 +101,43 @@ def tile_proto_t_kernel(tc, feature_map, weight2, scale, out):
                         wt[g][:, u, t * P : (t + 1) * P], ww[:, t * 256 + u : (t + 1) * 256 : 2], ident[:]
                     )
 
+        def split(g):
+            if g < 1 or g >= NSTEP:
+                return IMG
+            return IMG - (1 if g < HALF else 1)
+
+        def split_x(g):
+            n = IMG - split(g)
+            if n == 0:
+                return
+            xd[g] = dpool.tile([P, n * 512], F32, name="xd", tag=f"xd{n}")
+            nc.vector.tensor_copy(
+                out=xd[g][:].rearrange("p (j u w) -> p j u w", j=2 * n, u=2),
+                in_=xs[g][:, (IMG - n) * 1024 : IMG * 1024].bitcast(F32).rearrange("p (j w u) -> p j u w", j=2 * n, u=2),
+            )
+
         def transp_x(g, i):
-            if g >= NSTEP:
+            if g < 0 or g >= NSTEP:
                 return
             xw = xs[g][:].bitcast(F32)
             xt[g, i] = psum.tile([P, 2, IMG, 2, 32], F32, name="xt", tag="xt", bufs=4)
             for j in range(2):
                 for u in range(2):
-                    c0 = i * 512 + j * 256
-                    if (g, i) in xd:
-                        words = xd[g, i][:, (2 * j + u) * P : (2 * j + u + 1) * P]
+                    if i >= split(g):
+                        c0 = ((i - split(g)) * 4 + j * 2 + u) * P
+                        words = xd[g][:, c0 : c0 + P]
                     else:
+                        c0 = i * 512 + j * 256
                         words = xw[:, c0 + u : c0 + 256 : 2]
                     nc.tensor.transpose(
                         xt[g, i][:, u, :, j, :], words, ident[:].rearrange("p (i c) -> p i c", i=IMG)
                     )
 
-        def split_x(g):
-            if g < 1 or g >= NSTEP:
-                return
-            for i in SPLIT:
-                xd[g, i] = dpool.tile([P, 512], F32, name="xd", tag=f"xd{i}")
-                nc.vector.tensor_copy(
-                    out=xd[g, i][:].rearrange("p (j u w) -> p j u w", j=2, u=2),
-                    in_=xs[g][:, i * 1024 : (i + 1) * 1024].bitcast(F32).rearrange("p (j w u) -> p j u w", j=2, u=2),
-                )
-
         def copy_x(g, i, on_vector):
+            if g < 0 or g >= NSTEP:
+                return
+            if g not in gx:
+                gx[g] = work.tile([P, IMG * 1024], BF16, name="gx", tag="gx", align_bytes=64)
             dst = gx[g][:].bitcast(F32).rearrange("p (i b c u) -> p i b c u", i=IMG, b=IMG, c=64, u=2)[:, :, i, :, :]
             src = xt[g, i][:].rearrange("p u i r c -> p i (r c) u")
             if on_vector:
@@ -152,71 +148,68 @@ def tile_proto_t_kernel(tc, feature_map, weight2, scale, out):
         def copies_w(g):
             if g < 0 or g >= HALF:
                 return
-            ga[g] = work.tile([P, 1024], BF16, name="ga", tag="ga", align_bytes=64)
+            if g % 2 == 0:
+                ga[g // 2] = work.tile([P, 2048], BF16, name="ga", tag="ga", align_bytes=64)
             nc.vector.tensor_copy(
-                out=ga[g][:].bitcast(F32).rearrange("p (c r u) -> p c r u", r=2, u=2),
+                out=ga[g // 2][:, (g % 2) * 1024 : (g % 2 + 1) * 1024].bitcast(F32).rearrange("p (c r u) -> p c r u", r=2, u=2),
                 in_=wt[g][:].rearrange("p u (r c) -> p c r u", r=2),
             )
 
-        def copies_x(g):
-            if g >= NSTEP:
-                return
-            gx[g] = work.tile([P, IMG * 1024], BF16, name="gx", tag="gx", align_bytes=64)
-            for i in range(IMG):
-                if g == NSTEP - 1:
-                    copy_x(g, i, i % 2 == 1)
-                else:
-                    copy_x(g, i, False)
-
-        def quant_wa(g):
-            if g < 0 or g >= HALF:
-                return
-            nc.vector.quantize_mx(
-                out=wac[:, 256 * g : 256 * (g + 1)].bitcast(FP8X4), scales=was[:, 256 * g : 256 * (g + 1)], in_=ga[g][:]
-            )
-
         def move_w(g):
-            if g < HALF or g >= NSTEP:
+            if g < HALF or g >= NSTEP or g % 2:
                 return
             h = g - HALF
+            b = (h // 2) % 2
             nc.vector.tensor_copy(
-                out=wqc[h % 2][:, 0 : IMG * NS].bitcast(I32).rearrange("p (q s) -> p q s", q=IMG),
-                in_=wac[:, 0 : NS * NQ].bitcast(I32).rearrange("p (s q) -> p q s", s=NS)[:, IMG * h : IMG * (h + 1), :],
+                out=wqc[b][:, 0 : 2 * IMG * NS].bitcast(I32).rearrange("p (q s) -> p q s", q=2 * IMG),
+                in_=wac[:, 0 : NS * NQ].bitcast(I32).rearrange("p (s q) -> p q s", s=NS)[:, IMG * h : IMG * (h + 2), :],
             )
             nc.vector.tensor_copy(
-                out=wqs[h % 2][:, 0 : IMG * NS].rearrange("p (q s) -> p q s", q=IMG),
-                in_=was[:, 0 : NS * NQ].rearrange("p (s q) -> p q s", s=NS)[:, IMG * h : IMG * (h + 1), :],
+                out=wqs[b][:, 0 : 2 * IMG * NS].rearrange("p (q s) -> p q s", q=2 * IMG),
+                in_=was[:, 0 : NS * NQ].rearrange("p (s q) -> p q s", s=NS)[:, IMG * h : IMG * (h + 2), :],
             )
 
-        def quant_x(g):
+        def quant_wa(g):
+            if g < 0 or g >= HALF or g % 2 == 0:
+                return
+            c0 = 512 * (g // 2)
+            nc.vector.quantize_mx(
+                out=wac[:, c0 : c0 + 512].bitcast(FP8X4), scales=was[:, c0 : c0 + 512], in_=ga[g // 2][:]
+            )
+
+        def quant_x(g, a=None):
             if g < 0 or g >= NSTEP:
                 return
-            xc[g] = work.tile([P, IMG * 256], U32, name="xc", tag="xc", align_bytes=64)
-            xsc[g] = work.tile([P, IMG * 256], U8, name="xsc", tag="xsc", align_bytes=64)
-            pieces = 1
-            wid = IMG * 256 // pieces
-            for h in range(pieces):
+            if a is not None:
+                if a == 0:
+                    xc[g] = work.tile([P, IMG * 256], U32, name="xc", tag="xc", align_bytes=64, bufs=6)
+                    xsc[g] = work.tile([P, IMG * 256], U8, name="xsc", tag="xsc", align_bytes=64, bufs=6)
                 nc.vector.quantize_mx(
-                    out=xc[g][:, h * wid : (h + 1) * wid].bitcast(FP8X4),
-                    scales=xsc[g][:, h * wid : (h + 1) * wid],
-                    in_=gx[g][:, 4 * h * wid : 4 * (h + 1) * wid],
+                    out=xc[g][:, a * 512 : (a + 1) * 512].bitcast(FP8X4),
+                    scales=xsc[g][:, a * 512 : (a + 1) * 512],
+                    in_=gx[g][:, a * 2048 : (a + 1) * 2048],
                 )
+                return
+            xc[g] = work.tile([P, IMG * 256], U32, name="xc", tag="xc", align_bytes=64, bufs=6)
+            xsc[g] = work.tile([P, IMG * 256], U8, name="xsc", tag="xsc", align_bytes=64, bufs=6)
+            nc.vector.quantize_mx(out=xc[g][:].bitcast(FP8X4), scales=xsc[g][:], in_=gx[g][:])
 
-        def mx(g):
+        def mx(g, a=None):
             if g < 0 or g >= NSTEP:
                 return
-            mm[g] = psum.tile([P, 512], F32, name="mm", tag="mm", bufs=2)
-            for slot in range(8):
+            if a != 1:
+                mm[g] = psum.tile([P, 512], F32, name="mm", tag="mm", bufs=2)
+            for slot in range(8) if a is None else range(4 * a, 4 * a + 4):
                 if g < HALF:
                     j, i = slot // IMG, slot % IMG
                     codes, planes = wac, was
                     w0 = (IMG * g + i) * 64
                 else:
                     i, j = (slot // 4) * 2 + slot % 2, (slot // 2) % 2
-                    codes, planes = wqc[g % 2], wqs[g % 2]
-                    w0 = i * 64
+                    codes, planes = wqc[(g // 2) % 2], wqs[(g // 2) % 2]
+                    w0 = (IMG * (g % 2) + i) * 64
                 c0 = i * 256 + j * P
-                n = WIDTHS[slot]
+                n = 64 if i == IMG - 1 else 128
                 nc.tensor.matmul_mx(
                     out=mm[g][:, slot * 64 : slot * 64 + n],
                     lhsT=xc[g][:, c0 : c0 + P].bitcast(FP8X4),
@@ -235,10 +228,20 @@ def tile_proto_t_kernel(tc, feature_map, weight2, scale, out):
                 in_=mm[g][:].rearrange("p (j i q) -> p j q i", j=2, i=IMG, q=NQ),
             )
 
-        def sub(g):
+        def sub(g, a=None):
             if g < HALF or g >= NSTEP:
                 return
             h = g - HALF
+            if a is not None:
+                if a == 0:
+                    diff[g] = work.tile([P, 512], F32, name="diff", tag="diff")
+                nc.vector.tensor_tensor(
+                    out=diff[g][:, a * 256 : (a + 1) * 256].rearrange("p (j f) -> p j f", j=2),
+                    in0=mm[g][:, a * 256 : (a + 1) * 256].rearrange("p (j f) -> p j f", j=2),
+                    in1=csb4[:, :, IMG * h + 2 * a : IMG * h + 2 * a + 2, :].rearrange("p j b s -> p j (b s)"),
+                    op=ALU.subtract,
+                )
+                return
             diff[g] = work.tile([P, 512], F32, name="diff", tag="diff")
             nc.vector.tensor_tensor(
                 out=diff[g][:].rearrange("p (a j f) -> p a j f", a=2, j=2),
@@ -247,18 +250,19 @@ def tile_proto_t_kernel(tc, feature_map, weight2, scale, out):
                 op=ALU.subtract,
             )
 
-        def dtr(g):
+        def dtr(g, a=None):
             if g < HALF or g >= NSTEP:
                 return
-            dt[g] = psum.tile([P, 512], F32, name="dt", tag="aux", bufs=2)
-            for b in range(4):
+            if a != 1:
+                dt[g] = psum.tile([P, 512], F32, name="dt", tag="aux", bufs=2)
+            for b in range(4) if a is None else (2 * a, 2 * a + 1):
                 nc.tensor.transpose(dt[g][:, b * P : (b + 1) * P], diff[g][:, b * P : (b + 1) * P], ident[:])
 
-        def sq(g):
+        def sq(g, half=None):
             if g < HALF or g >= NSTEP:
                 return
             h = g - HALF
-            for a in range(2):
+            for a in range(2) if half is None else (half,):
                 junk = work.tile([P, 256], F32, name="junk", tag="junk")
                 nc.scalar.activation(
                     out=junk[:],
@@ -267,30 +271,61 @@ def tile_proto_t_kernel(tc, feature_map, weight2, scale, out):
                     accum_out=l2col[:, 2 * h + a : 2 * h + a + 1],
                 )
 
-        if PIN:
-            ctx.enter_context(tc.manual_schedule())
-
+        ctx.enter_context(tc.manual_schedule())
         for g in range(LOOKAHEAD):
             load(g)
-        for k in range(NSTEP + 6):
-            load(k + LOOKAHEAD)
-            copies_w(k - 1)
-            split_x(k + 1)
-            sub(k - 3)
-            quant_x(k - 1)
-            quant_wa(k - 1)
-            move_w(k - 1)
-            sq(k - 5)
-            ccopy(k - 3)
-            dtr(k - 4)
-            if k == 0:
-                transp_x(0, 0)
-            transp_w(k)
-            for i in range(1 if k == 0 else 0, IMG):
-                transp_x(k, i)
-            mx(k - 2)
-            copies_x(k)
+        def front(g):
+            ccopy(g - 4)
+            sub(g - 4)
+            sq(g - 6)
+            dtr(g - 5)
+            copies_w(g - 1)
+            transp_w(g)
+            quant_x(g - 1)
+            split_x(g + 1)
+            for i in range(IMG):
+                transp_x(g, i)
+                copy_x(g, i, i == 3 and g % 2 == 1)
+            quant_wa(g - 1)
+            move_w(g)
 
+        n = NSTEP - 1
+        for k in range(0, NSTEP, 2):
+            load(k + LOOKAHEAD)
+            load(k + 1 + LOOKAHEAD)
+            mx(k - 4)
+            mx(k - 3)
+            front(k)
+            if k + 1 == n:
+                mx(n - 3)
+            front(k + 1)
+        mx(n - 2)
+        dtr(n - 4)
+        sq(n - 5)
+        sub(n - 3)
+        quant_x(n, 0)
+        quant_x(n, 1)
+        mx(n - 1)
+        sq(n - 4)
+        sub(n - 2)
+        dtr(n - 3)
+        mx(n, 0)
+        mx(n, 1)
+        sub(n - 1)
+        sq(n - 3)
+        dtr(n - 2)
+        sub(n, 0)
+        sub(n, 1)
+        sq(n - 2)
+        dtr(n - 1)
+        sq(n - 1)
+        dtr(n, 0)
+        dtr(n, 1)
+        sq(n, 0)
+        sq(n, 1)
+
+        a_sb = const.tile([P, 1], F32)
+        nc.vector.tensor_scalar_mul(a_sb[:], sc_bf[:], -1.0 / (800.0 * M * M))
         l2t = psum.tile([P, P], F32, name="l2t", tag="aux", bufs=2)
         nc.tensor.transpose(l2t[:], l2col[:], ident[:])
         lg = const.tile([P, 2, NS], F32)

@@ -148,10 +148,9 @@ def tile_proto_t_kernel(tc, feature_map, weight2, scale, out):
         def copies_w(g):
             if g < 0 or g >= HALF:
                 return
-            if g % 2 == 0:
-                ga[g // 2] = work.tile([P, 2048], BF16, name="ga", tag="ga", align_bytes=64)
+            ga[g] = work.tile([P, 1024], BF16, name="ga", tag="ga", align_bytes=64)
             nc.vector.tensor_copy(
-                out=ga[g // 2][:, (g % 2) * 1024 : (g % 2 + 1) * 1024].bitcast(F32).rearrange("p (c r u) -> p c r u", r=2, u=2),
+                out=ga[g][:].bitcast(F32).rearrange("p (c r u) -> p c r u", r=2, u=2),
                 in_=wt[g][:].rearrange("p u (r c) -> p c r u", r=2),
             )
 
@@ -170,11 +169,11 @@ def tile_proto_t_kernel(tc, feature_map, weight2, scale, out):
             )
 
         def quant_wa(g):
-            if g < 0 or g >= HALF or g % 2 == 0:
+            if g < 0 or g >= HALF:
                 return
-            c0 = 512 * (g // 2)
+            c0 = 256 * g
             nc.vector.quantize_mx(
-                out=wac[:, c0 : c0 + 512].bitcast(FP8X4), scales=was[:, c0 : c0 + 512], in_=ga[g // 2][:]
+                out=wac[:, c0 : c0 + 256].bitcast(FP8X4), scales=was[:, c0 : c0 + 256], in_=ga[g][:]
             )
 
         def quant_x(g, a=None):
@@ -275,10 +274,11 @@ def tile_proto_t_kernel(tc, feature_map, weight2, scale, out):
         for g in range(LOOKAHEAD):
             load(g)
         def front(g):
-            ccopy(g - 4)
-            sub(g - 4)
-            sq(g - 6)
-            dtr(g - 5)
+            mx(g - 3)
+            ccopy(g - 3)
+            sub(g - 3)
+            sq(g - 5)
+            dtr(g - 4)
             copies_w(g - 1)
             transp_w(g)
             quant_x(g - 1)
@@ -290,25 +290,16 @@ def tile_proto_t_kernel(tc, feature_map, weight2, scale, out):
             move_w(g)
 
         n = NSTEP - 1
-        for k in range(0, NSTEP, 2):
+        for k in range(NSTEP):
             load(k + LOOKAHEAD)
-            load(k + 1 + LOOKAHEAD)
-            mx(k - 4)
-            mx(k - 3)
             front(k)
-            if k + 1 == n:
-                mx(n - 3)
-            front(k + 1)
         mx(n - 2)
-        dtr(n - 4)
-        sq(n - 5)
-        sub(n - 3)
+        dtr(n - 3)
+        sq(n - 4)
+        sub(n - 2)
         quant_x(n, 0)
         quant_x(n, 1)
         mx(n - 1)
-        sq(n - 4)
-        sub(n - 2)
-        dtr(n - 3)
         mx(n, 0)
         mx(n, 1)
         sub(n - 1)

@@ -104,7 +104,7 @@ def tile_proto_t_kernel(tc, feature_map, weight2, scale, out):
         def split(g):
             if g < 1 or g >= NSTEP:
                 return IMG
-            return IMG - (1 if g < HALF else 1)
+            return IMG - (2 if g < HALF else 1)
 
         def split_x(g):
             n = IMG - split(g)
@@ -277,15 +277,15 @@ def tile_proto_t_kernel(tc, feature_map, weight2, scale, out):
             mx(g - 3)
             ccopy(g - 3)
             sub(g - 3)
-            sq(g - 5)
-            dtr(g - 4)
             copies_w(g - 1)
             transp_w(g)
             quant_x(g - 1)
             split_x(g + 1)
             for i in range(IMG):
                 transp_x(g, i)
-                copy_x(g, i, i == 3 and g % 2 == 1)
+                copy_x(g, i, i == 3 and g % (4 if g < HALF else 2) == 1)
+            dtr(g - 3)
+            sq(g - 3)
             quant_wa(g - 1)
             move_w(g)
 
@@ -294,25 +294,22 @@ def tile_proto_t_kernel(tc, feature_map, weight2, scale, out):
             load(k + LOOKAHEAD)
             front(k)
         mx(n - 2)
-        dtr(n - 3)
-        sq(n - 4)
+        mx(n - 1)
         sub(n - 2)
         quant_x(n, 0)
         quant_x(n, 1)
-        mx(n - 1)
+        dtr(n - 2)
+        sq(n - 2)
         mx(n, 0)
         mx(n, 1)
         sub(n - 1)
-        sq(n - 3)
-        dtr(n - 2)
-        sub(n, 0)
-        sub(n, 1)
-        sq(n - 2)
         dtr(n - 1)
         sq(n - 1)
+        sub(n, 0)
+        sub(n, 1)
         dtr(n, 0)
-        dtr(n, 1)
         sq(n, 0)
+        dtr(n, 1)
         sq(n, 1)
 
         a_sb = const.tile([P, 1], F32)

@@ -84,9 +84,12 @@ def tile_proto_t_kernel(tc, feature_map, weight2, scale, out):
                     out=ws[g][:],
                     in_=weight2[IMG * g : IMG * (g + 1)].rearrange("s q m -> (s q) m").rearrange("(p r) m -> p (r m)", r=2),
                 )
-            if g == 0:
-                for i in range(1, IMG):
+            if g < 1:
+                for i in range(1 if g == 0 else 0, IMG):
                     nc.sync.dma_start(out=dst[:, i, :], in_=src[:, i, :])
+            elif g < 4:
+                for i in range(0, IMG, 2):
+                    nc.sync.dma_start(out=dst[:, i : i + 2, :], in_=src[:, i : i + 2, :])
             else:
                 nc.sync.dma_start(out=xs[g][:], in_=rows.rearrange("(p r) m -> p (r m)", r=2 * IMG))
 
@@ -102,7 +105,7 @@ def tile_proto_t_kernel(tc, feature_map, weight2, scale, out):
                     )
 
         def split(g):
-            if g < 1 or g >= NSTEP:
+            if g < 4 or g >= NSTEP:
                 return IMG
             return IMG - (2 if g < HALF else 1)
 
@@ -280,13 +283,13 @@ def tile_proto_t_kernel(tc, feature_map, weight2, scale, out):
             copies_w(g - 1)
             transp_w(g)
             quant_x(g - 1)
+            quant_wa(g - 1)
             split_x(g + 1)
             for i in range(IMG):
                 transp_x(g, i)
                 copy_x(g, i, i == 3 and g % (4 if g < HALF else 2) == 1)
             dtr(g - 3)
             sq(g - 3)
-            quant_wa(g - 1)
             move_w(g)
 
         n = NSTEP - 1
@@ -313,21 +316,23 @@ def tile_proto_t_kernel(tc, feature_map, weight2, scale, out):
         sq(n, 1)
 
         a_sb = const.tile([P, 1], F32)
-        nc.vector.tensor_scalar_mul(a_sb[:], sc_bf[:], -1.0 / (800.0 * M * M))
+        nc.vector.tensor_scalar_mul(a_sb[:], sc_bf[:], 1.0 / (800.0 * M * M))
         l2t = psum.tile([P, P], F32, name="l2t", tag="aux", bufs=2)
         nc.tensor.transpose(l2t[:], l2col[:], ident[:])
-        lg = const.tile([P, 2, NS], F32)
-        nc.vector.tensor_scalar_mul(lg[:].rearrange("p a s -> p (a s)"), l2t[:], a_sb[:, 0:1])
-        top = const.tile([P, 2], F32)
-        nc.vector.tensor_reduce(out=top[:], in_=lg[:], axis=AX.X, op=ALU.max)
-        z = const.tile([P, 2, NS], F32)
-        nc.vector.tensor_tensor(
-            out=z[:], in0=lg[:], in1=top[:].unsqueeze(2).to_broadcast([P, 2, NS]), op=ALU.subtract
-        )
+        neg = const.tile([P, 2, NS], F32)
+        nc.vector.tensor_scalar_mul(neg[:].rearrange("p a s -> p (a s)"), l2t[:], a_sb[:, 0:1])
+        low = const.tile([P, 2], F32)
+        nc.vector.tensor_reduce(out=low[:], in_=neg[:], axis=AX.X, op=ALU.min)
         ez = const.tile([P, 2, NS], F32)
         tot = const.tile([P, 2], F32)
         for a in range(2):
-            nc.scalar.activation(out=ez[:, a, :], in_=z[:, a, :], func=ACT.Exp, accum_out=tot[:, a : a + 1])
+            nc.scalar.activation(
+                out=ez[:, a, :], in_=neg[:, a, :], func=ACT.Exp, scale=-1.0, bias=low[:, a : a + 1], accum_out=tot[:, a : a + 1]
+            )
+        z = const.tile([P, 2, NS], F32)
+        nc.vector.tensor_tensor(
+            out=z[:], in0=low[:].unsqueeze(2).to_broadcast([P, 2, NS]), in1=neg[:], op=ALU.subtract
+        )
         ltot = const.tile([P, 2], F32)
         nc.scalar.activation(out=ltot[:], in_=tot[:], func=ACT.Ln)
         res = const.tile([P, 2, NS], F32)

@@ -285,7 +285,7 @@ def tile_proto_t_kernel(tc, feature_map, weight2, scale, out):
             quant_x(g - 1)
             quant_wa(g - 1)
             split_x(g + 1)
-            for i in range(IMG):
+            for i in (0, 2, 1, 3):
                 transp_x(g, i)
                 copy_x(g, i, i == 3 and g % (4 if g < HALF else 2) == 1)
             dtr(g - 3)

@@ -201,7 +201,8 @@ def tile_proto_t_kernel(tc, feature_map, weight2, scale, out):
                 return
             if a != 1:
                 mm[g] = psum.tile([P, 512], F32, name="mm", tag="mm", bufs=2)
-            for slot in range(8) if a is None else range(4 * a, 4 * a + 4):
+            first, last = (0, 7) if a is None else (4 * a, 4 * a + 3)
+            for slot in range(last, first - 1, -1):
                 if g < HALF:
                     j, i = slot // IMG, slot % IMG
                     codes, planes = wac, was
@@ -211,13 +212,13 @@ def tile_proto_t_kernel(tc, feature_map, weight2, scale, out):
                     codes, planes = wqc[(g // 2) % 2], wqs[(g // 2) % 2]
                     w0 = (IMG * (g % 2) + i) * 64
                 c0 = i * 256 + j * P
-                n = 64 if i == IMG - 1 else 128
+                reach = 0 if slot == first or w0 == 0 else 64
                 nc.tensor.matmul_mx(
-                    out=mm[g][:, slot * 64 : slot * 64 + n],
+                    out=mm[g][:, slot * 64 - reach : slot * 64 + 64],
                     lhsT=xc[g][:, c0 : c0 + P].bitcast(FP8X4),
                     lhsT_scale=xsc[g][:, c0 : c0 + P],
-                    rhs=codes[:, w0 : w0 + n].bitcast(FP8X4),
-                    rhs_scale=planes[:, w0 : w0 + n],
+                    rhs=codes[:, w0 - reach : w0 + 64].bitcast(FP8X4),
+                    rhs_scale=planes[:, w0 - reach : w0 + 64],
                     start=True,
                     stop=True,
                 )

from contextlib import ExitStack

import concourse.mybir as mybir
from concourse.masks import make_identity

F32 = mybir.dt.float32
BF16 = mybir.dt.bfloat16
U32 = mybir.dt.uint32
U8 = mybir.dt.uint8
I32 = mybir.dt.int32
FP8X4 = mybir.dt.float8_e4m3fn_x4
ACT = mybir.ActivationFunctionType
ALU = mybir.AluOpType
AX = mybir.AxisListType

P = 128
NS = 64
NQ = 64
D = 256
M = 512
FLOPS = 2 * 2 * NS * NQ * D * M

IMG = 4
NSTEP = (NS + NQ) // IMG
HALF = NS // IMG
LOOKAHEAD = 5


def tile_proto_t_kernel(tc, feature_map, weight2, scale, out):
    nc = tc.nc
    with ExitStack() as ctx:
        const = ctx.enter_context(tc.tile_pool(name="const", bufs=1))
        xpool = ctx.enter_context(tc.tile_pool(name="xpool", bufs=LOOKAHEAD + 2))
        dpool = ctx.enter_context(tc.tile_pool(name="dpool", bufs=3))
        wpool = ctx.enter_context(tc.tile_pool(name="wpool", bufs=LOOKAHEAD + 2))
        work = ctx.enter_context(tc.tile_pool(name="work", bufs=3))
        psum = ctx.enter_context(tc.psum_pool(name="psum", bufs=2))

        ident = const.tile([P, P], F32)
        make_identity(nc, ident[:])
        sc_bf = const.tile([P, 1], BF16)
        nc.scalar.dma_start(out=sc_bf[:], in_=scale.partition_broadcast(P))
        l2col = const.tile([P, P], F32)
        nc.vector.memset(l2col[:], 0.0)
        warm = const.tile([P, 1], F32)
        nc.scalar.activation(out=warm[:], in_=l2col[:, 0:1], func=ACT.Exp)

        csb = const.tile([P, 2 * NQ * NS], F32)
        csb4 = csb[:].rearrange("p (j q s) -> p j q s", j=2, q=NQ, s=NS)
        wac = const.tile([P, NQ * NS], U32, align_bytes=64)
        was = const.tile([P, NQ * NS], U8, align_bytes=64)
        wqc0 = const.tile([P, 2 * IMG * NS], U32, align_bytes=64)
        wqs0 = const.tile([P, 2 * IMG * NS], U8, align_bytes=64)
        wqc1 = const.tile([P, 2 * IMG * NS], U32, align_bytes=64)
        wqs1 = const.tile([P, 2 * IMG * NS], U8, align_bytes=64)
        wqc = (wqc0, wqc1)
        wqs = (wqs0, wqs1)

        xs = {}
        xd = {}
        ws = {}
        xt = {}
        wt = {}
        gx = {}
        ga = {}
        xc = {}
        xsc = {}
        mm = {}
        diff = {}
        dt = {}

        def load(g):
            if g >= NSTEP:
                return
            xs[g] = xpool.tile([P, IMG * 1024], BF16, name="xs", tag="xs")
            dst = xs[g][:].rearrange("p (b f) -> p b f", b=IMG)
            rows = feature_map[IMG * g : IMG * (g + 1)].rearrange("i d m -> (i d) m")
            src = rows.rearrange("(p b r) m -> p b (r m)", b=IMG, r=2)
            if g == 0:
                nc.sync.dma_start(out=dst[:, 0, :], in_=src[:, 0, :])
            if g < HALF:
                ws[g] = wpool.tile([P, 2 * M], BF16, name="ws", tag="ws")
                nc.sync.dma_start(
                    out=ws[g][:],
                    in_=weight2[IMG * g : IMG * (g + 1)].rearrange("s q m -> (s q) m").rearrange("(p r) m -> p (r m)", r=2),
                )
            if g < 1:
                for i in range(1 if g == 0 else 0, IMG):
                    nc.sync.dma_start(out=dst[:, i, :], in_=src[:, i, :])
            elif g < 4:
                for i in range(0, IMG, 2):
                    nc.sync.dma_start(out=dst[:, i : i + 2, :], in_=src[:, i : i + 2, :])
            else:
                nc.sync.dma_start(out=xs[g][:], in_=rows.rearrange("(p r) m -> p (r m)", r=2 * IMG))

        def transp_w(g):
            if g < 0 or g >= HALF:
                return
            wt[g] = psum.tile([P, 2, 256], F32, name="wt", tag="aux", bufs=2)
            ww = ws[g][:].bitcast(F32)
            for t in range(2):
                for u in range(2):
                    nc.tensor.transpose(
                        wt[g][:, u, t * P : (t + 1) * P], ww[:, t * 256 + u : (t + 1) * 256 : 2], ident[:]
                    )

        def split(g):
            if g < 4 or g >= NSTEP:
                return IMG
            return IMG - (2 if g < HALF else 1)

        def split_x(g):
            n = IMG - split(g)
            if n == 0:
                return
            xd[g] = dpool.tile([P, n * 512], F32, name="xd", tag=f"xd{n}")
            nc.vector.tensor_copy(
                out=xd[g][:].rearrange("p (j u w) -> p j u w", j=2 * n, u=2),
                in_=xs[g][:, (IMG - n) * 1024 : IMG * 1024].bitcast(F32).rearrange("p (j w u) -> p j u w", j=2 * n, u=2),
            )

        def transp_x(g, i):
            if g < 0 or g >= NSTEP:
                return
            xw = xs[g][:].bitcast(F32)
            xt[g, i] = psum.tile([P, 2, IMG, 2, 32], F32, name="xt", tag="xt", bufs=4)
            for j in range(2):
                for u in range(2):
                    if i >= split(g):
                        c0 = ((i - split(g)) * 4 + j * 2 + u) * P
                        words = xd[g][:, c0 : c0 + P]
                    else:
                        c0 = i * 512 + j * 256
                        words = xw[:, c0 + u : c0 + 256 : 2]
                    nc.tensor.transpose(
                        xt[g, i][:, u, :, j, :], words, ident[:].rearrange("p (i c) -> p i c", i=IMG)
                    )

        def copy_x(g, i, on_vector):
            if g < 0 or g >= NSTEP:
                return
            if g not in gx:
                gx[g] = work.tile([P, IMG * 1024], BF16, name="gx", tag="gx", align_bytes=64)
            dst = gx[g][:].bitcast(F32).rearrange("p (i b c u) -> p i b c u", i=IMG, b=IMG, c=64, u=2)[:, :, i, :, :]
            src = xt[g, i][:].rearrange("p u i r c -> p i (r c) u")
            if on_vector:
                nc.vector.tensor_copy(out=dst, in_=src)
            else:
                nc.scalar.copy(out=dst, in_=src)

        def copies_w(g):
            if g < 0 or g >= HALF:
                return
            ga[g] = work.tile([P, 1024], BF16, name="ga", tag="ga", align_bytes=64)
            nc.vector.tensor_copy(
                out=ga[g][:].bitcast(F32).rearrange("p (c r u) -> p c r u", r=2, u=2),
                in_=wt[g][:].rearrange("p u (r c) -> p c r u", r=2),
            )

        def move_w(g):
            if g < HALF or g >= NSTEP or g % 2:
                return
            h = g - HALF
            b = (h // 2) % 2
            nc.vector.tensor_copy(
                out=wqc[b][:, 0 : 2 * IMG * NS].bitcast(I32).rearrange("p (q s) -> p q s", q=2 * IMG),
                in_=wac[:, 0 : NS * NQ].bitcast(I32).rearrange("p (s q) -> p q s", s=NS)[:, IMG * h : IMG * (h + 2), :],
            )
            nc.vector.tensor_copy(
                out=wqs[b][:, 0 : 2 * IMG * NS].rearrange("p (q s) -> p q s", q=2 * IMG),
                in_=was[:, 0 : NS * NQ].rearrange("p (s q) -> p q s", s=NS)[:, IMG * h : IMG * (h + 2), :],
            )

        def quant_wa(g):
            if g < 0 or g >= HALF:
                return
            c0 = 256 * g
            nc.vector.quantize_mx(
                out=wac[:, c0 : c0 + 256].bitcast(FP8X4), scales=was[:, c0 : c0 + 256], in_=ga[g][:]
            )

        def quant_x(g, a=None):
            if g < 0 or g >= NSTEP:
                return
            if a is not None:
                if a == 0:
                    xc[g] = work.tile([P, IMG * 256], U32, name="xc", tag="xc", align_bytes=64, bufs=6)
                    xsc[g] = work.tile([P, IMG * 256], U8, name="xsc", tag="xsc", align_bytes=64, bufs=6)
                nc.vector.quantize_mx(
                    out=xc[g][:, a * 512 : (a + 1) * 512].bitcast(FP8X4),
                    scales=xsc[g][:, a * 512 : (a + 1) * 512],
                    in_=gx[g][:, a * 2048 : (a + 1) * 2048],
                )
                return
            xc[g] = work.tile([P, IMG * 256], U32, name="xc", tag="xc", align_bytes=64, bufs=6)
            xsc[g] = work.tile([P, IMG * 256], U8, name="xsc", tag="xsc", align_bytes=64, bufs=6)
            nc.vector.quantize_mx(out=xc[g][:].bitcast(FP8X4), scales=xsc[g][:], in_=gx[g][:])

        def mx(g, a=None):
            if g < 0 or g >= NSTEP:
                return
            if a != 1:
                mm[g] = psum.tile([P, 512], F32, name="mm", tag="mm", bufs=2)
            first, last = (0, 7) if a is None else (4 * a, 4 * a + 3)
            for slot in range(last, first - 1, -1):
                if g < HALF:
                    j, i = slot // IMG, slot % IMG
                    codes, planes = wac, was
                    w0 = (IMG * g + i) * 64
                else:
                    i, j = (slot // 4) * 2 + slot % 2, (slot // 2) % 2
                    codes, planes = wqc[(g // 2) % 2], wqs[(g // 2) % 2]
                    w0 = (IMG * (g % 2) + i) * 64
                c0 = i * 256 + j * P
                reach = 0 if slot == first or w0 == 0 else 64
                nc.tensor.matmul_mx(
                    out=mm[g][:, slot * 64 - reach : slot * 64 + 64],
                    lhsT=xc[g][:, c0 : c0 + P].bitcast(FP8X4),
                    lhsT_scale=xsc[g][:, c0 : c0 + P],
                    rhs=codes[:, w0 - reach : w0 + 64].bitcast(FP8X4),
                    rhs_scale=planes[:, w0 - reach : w0 + 64],
                    start=True,
                    stop=True,
                )

        def ccopy(g):
            if g < 0 or g >= HALF:
                return
            nc.scalar.copy(
                out=csb4[:, :, :, IMG * g : IMG * (g + 1)],
                in_=mm[g][:].rearrange("p (j i q) -> p j q i", j=2, i=IMG, q=NQ),
            )

        def sub(g, a=None):
            if g < HALF or g >= NSTEP:
                return
            h = g - HALF
            if a is not None:
                if a == 0:
                    diff[g] = work.tile([P, 512], F32, name="diff", tag="diff")
                nc.vector.tensor_tensor(
                    out=diff[g][:, a * 256 : (a + 1) * 256].rearrange("p (j f) -> p j f", j=2),
                    in0=mm[g][:, a * 256 : (a + 1) * 256].rearrange("p (j f) -> p j f", j=2),
                    in1=csb4[:, :, IMG * h + 2 * a : IMG * h + 2 * a + 2, :].rearrange("p j b s -> p j (b s)"),
                    op=ALU.subtract,
                )
                return
            diff[g] = work.tile([P, 512], F32, name="diff", tag="diff")
            nc.vector.tensor_tensor(
                out=diff[g][:].rearrange("p (a j f) -> p a j f", a=2, j=2),
                in0=mm[g][:].rearrange("p (a j f) -> p a j f", a=2, j=2),
                in1=csb4[:, :, IMG * h : IMG * (h + 1), :].rearrange("p j (a b) s -> p a j (b s)", a=2, b=2),
                op=ALU.subtract,
            )

        def dtr(g, a=None):
            if g < HALF or g >= NSTEP:
                return
            if a != 1:
                dt[g] = psum.tile([P, 512], F32, name="dt", tag="aux", bufs=2)
            for b in range(4) if a is None else (2 * a, 2 * a + 1):
                nc.tensor.transpose(dt[g][:, b * P : (b + 1) * P], diff[g][:, b * P : (b + 1) * P], ident[:])

        def sq(g, half=None):
            if g < HALF or g >= NSTEP:
                return
            h = g - HALF
            for a in range(2) if half is None else (half,):
                junk = work.tile([P, 256], F32, name="junk", tag="junk")
                nc.scalar.activation(
                    out=junk[:],
                    in_=dt[g][:, a * 256 : (a + 1) * 256],
                    func=ACT.Square,
                    accum_out=l2col[:, 2 * h + a : 2 * h + a + 1],
                )

        ctx.enter_context(tc.manual_schedule())
        for g in range(LOOKAHEAD):
            load(g)
        def front(g):
            mx(g - 3)
            ccopy(g - 3)
            sub(g - 3)
            copies_w(g - 1)
            transp_w(g)
            quant_x(g - 1)
            quant_wa(g - 1)
            split_x(g + 1)
            for i in (0, 2, 1, 3):
                transp_x(g, i)
                copy_x(g, i, i == 3 and g % (4 if g < HALF else 2) == 1)
            dtr(g - 3)
            sq(g - 3)
            move_w(g)

        n = NSTEP - 1
        for k in range(NSTEP):
            load(k + LOOKAHEAD)
            front(k)
        mx(n - 2)
        mx(n - 1)
        sub(n - 2)
        quant_x(n, 0)
        quant_x(n, 1)
        dtr(n - 2)
        sq(n - 2)
        mx(n, 0)
        mx(n, 1)
        sub(n - 1)
        dtr(n - 1)
        sq(n - 1)
        sub(n, 0)
        sub(n, 1)
        dtr(n, 0)
        sq(n, 0)
        dtr(n, 1)
        sq(n, 1)

        a_sb = const.tile([P, 1], F32)
        nc.vector.tensor_scalar_mul(a_sb[:], sc_bf[:], 1.0 / (800.0 * M * M))
        l2t = psum.tile([P, P], F32, name="l2t", tag="aux", bufs=2)
        nc.tensor.transpose(l2t[:], l2col[:], ident[:])
        neg = const.tile([P, 2, NS], F32)
        nc.vector.tensor_scalar_mul(neg[:].rearrange("p a s -> p (a s)"), l2t[:], a_sb[:, 0:1])
        low = const.tile([P, 2], F32)
        nc.vector.tensor_reduce(out=low[:], in_=neg[:], axis=AX.X, op=ALU.min)
        ez = const.tile([P, 2, NS], F32)
        tot = const.tile([P, 2], F32)
        for a in range(2):
            nc.scalar.activation(
                out=ez[:, a, :], in_=neg[:, a, :], func=ACT.Exp, scale=-1.0, bias=low[:, a : a + 1], accum_out=tot[:, a : a + 1]
            )
        z = const.tile([P, 2, NS], F32)
        nc.vector.tensor_tensor(
            out=z[:], in0=low[:].unsqueeze(2).to_broadcast([P, 2, NS]), in1=neg[:], op=ALU.subtract
        )
        ltot = const.tile([P, 2], F32)
        nc.scalar.activation(out=ltot[:], in_=tot[:], func=ACT.Ln)
        res = const.tile([P, 2, NS], F32)
        nc.vector.tensor_tensor(
            out=res[:], in0=z[:], in1=ltot[:].unsqueeze(2).to_broadcast([P, 2, NS]), op=ALU.subtract
        )
        nc.sync.dma_start(
            out=out.rearrange("(u a) s -> u (a s)", a=2), in_=res[0:32].rearrange("p a s -> p (a s)")
        )
